import numpy as np
import ml_dtypes


BF16 = ml_dtypes.bfloat16


def bf(x):
    return np.asarray(x, np.float32).astype(BF16)


def f64(x):
    return np.asarray(x).astype(np.float64)


E2M1 = np.array([0.0, 0.5, 1.0, 1.5, 2.0, 3.0, 4.0, 6.0, -0.0, -0.5, -1.0, -1.5, -2.0, -3.0, -4.0, -6.0])


def pack_weight(w, fmt):
    k, n = w.shape
    w = f64(bf(w)).reshape(k // 32, 32, n)
    amax = np.abs(w).max(1)
    if fmt == "e4m3":
        byte = np.frexp(amax)[1] - 1 + 127 - 7
    else:
        mant, ex = np.frexp(amax / 6.0)
        byte = np.where(mant > 0.5, ex, ex - 1) + 127
    byte = np.clip(np.where(amax > 0, byte, 1), 1, 254)
    scaled = (w * np.exp2(127.0 - byte)[:, None, :]).reshape(k, n).astype(np.float32)
    by_word = np.ascontiguousarray(scaled.reshape(k // 512, 128, 4, n).transpose(0, 1, 3, 2))
    if fmt == "e4m3":
        words = by_word.astype(ml_dtypes.float8_e4m3fn).view(np.uint8)
    else:
        c = by_word.astype(ml_dtypes.float4_e2m1fn).view(np.uint8) & 0xF
        words = c[..., 0::2] | (c[..., 1::2] << 4)
    return np.ascontiguousarray(words), np.ascontiguousarray(byte.astype(np.uint8).reshape(k // 512, 16, n))


def unpack_weight(words, scales, fmt):
    g, p, n, _ = words.shape
    if fmt == "e4m3":
        vals = np.ascontiguousarray(words).view(ml_dtypes.float8_e4m3fn).astype(np.float64)
    else:
        nib = np.empty((g, p, n, 4), np.uint8)
        nib[..., 0::2] = words & 0xF
        nib[..., 1::2] = words >> 4
        vals = E2M1[nib]
    vals = vals * np.repeat(np.exp2(scales.astype(np.float64) - 127.0), 8, axis=1)[..., None]
    return vals.transpose(0, 1, 3, 2).reshape(g * 512, n)

def pack4(w):
    words, scales = pack_weight(w, "e2m1")
    return words.reshape(words.shape[0], 128, -1), scales


def unpack4(words, scales):
    return unpack_weight(words.reshape(words.shape[0], 128, -1, 2), scales, "e2m1")


def kspread(k):
    return np.exp2(np.repeat(np.random.randint(-6, 7, k // 32), 32).astype(np.float64))


B, S, C, E, H = 4, 384, 2048, 2048, 16
ROPE_BASE = 10000.0
NORM_EPS = 1e-12
INV_FREQ = ROPE_BASE ** (-(np.arange(0, E, 2) / E))
THETA = S * np.repeat(INV_FREQ, 2)
SIN, COS = np.sin(THETA), np.cos(THETA)


def rotate(t):
    t1 = t[..., :-1:2]
    t2 = t[..., 1::2]
    t_rot = np.concatenate((-t2, t1), axis=-1)
    return t * COS + t_rot * SIN


def l2_normalize(t):
    n = np.sqrt((t * t).sum(-1, keepdims=True))
    return t / np.maximum(n, NORM_EPS)


def setup_inputs():
    s = kspread(C)
    x = np.random.standard_normal((B, S, C)) * s
    x_words, x_scales = pack4(np.ascontiguousarray(x.reshape(B * S, C).T))
    w = np.random.standard_normal((3 * E, C)) / np.sqrt(C) / s
    words, scales = pack4(np.ascontiguousarray(w.T))
    bqkv = bf(np.random.standard_normal(3 * E) * 0.3)
    return {"x_words": x_words, "x_scales": x_scales, "Wqkv_words": words, "Wqkv_scales": scales, "bqkv": bqkv}


def reference(x_words, x_scales, Wqkv_words, Wqkv_scales, bqkv):
    xq = unpack4(x_words, x_scales).T.reshape(B, S, C)
    wq = unpack4(Wqkv_words, Wqkv_scales).T
    b = f64(bqkv)
    q = (xq @ wq[:E].T) + b[:E]
    k = (xq @ wq[E:2 * E].T) + b[E:2 * E]
    v = (xq @ wq[2 * E:].T) + b[2 * E:]
    return l2_normalize(rotate(q)), l2_normalize(rotate(k)), v

@@ -1,0 +1,354 @@
+import math
+from contextlib import ExitStack
+
+import concourse.mybir as mybir
+from concourse.masks import make_identity
+
+F32 = mybir.dt.float32
+BF16 = mybir.dt.bfloat16
+I32 = mybir.dt.int32
+U8 = mybir.dt.uint8
+FP4X4 = mybir.dt.float4_e2m1fn_x4
+MULT = mybir.AluOpType.mult
+ADD = mybir.AluOpType.add
+SUB = mybir.AluOpType.subtract
+ACT = mybir.ActivationFunctionType
+
+P = 128
+TOK = 1536
+SEQ = 384
+E = 2048
+G = 4
+NT = 512
+BANKS = E // NT
+TILES = TOK // P
+ROPE_BASE = 10000.0
+FLOPS = 2 * TOK * E * 3 * E
+
+HALF = E // 2
+TURN_RATIO = ROPE_BASE ** (-2.0 / E)
+REDUCED = 640
+X_CHUNKS = ((0, 256), (256, 1280))
+W_CHUNKS = ((0, 512), (512, 512), (1024, 1024), (2048, 1024), (3072, 1024), (4096, 1024), (5120, 1024))
+
+
+def tile_multiheadattention_pa_kernel(tc, x_words, x_scales, Wqkv_words, Wqkv_scales, bqkv, out_0, out_1, out_2):
+    nc = tc.nc
+    outs = [o.flatten_outer_dims() for o in (out_0, out_1, out_2)]
+    with ExitStack() as ctx:
+        keep = ctx.enter_context(tc.tile_pool(name="keep", bufs=1))
+        prod = ctx.enter_context(tc.tile_pool(name="prod", bufs=3))
+        zs = ctx.enter_context(tc.tile_pool(name="zs", bufs=4))
+        vs = ctx.enter_context(tc.tile_pool(name="vs", bufs=2))
+        junk = ctx.enter_context(tc.tile_pool(name="junk", bufs=1))
+        small = ctx.enter_context(tc.tile_pool(name="small", bufs=4))
+        fixed = ctx.enter_context(tc.psum_pool(name="fixed", bufs=1))
+        acc = ctx.enter_context(tc.psum_pool(name="acc", bufs=4))
+        ctx.enter_context(tc.manual_schedule())
+
+        x_codes, x_planes, w_codes, w_planes = [], [], [], []
+        for i, (c0, width) in enumerate(X_CHUNKS):
+            t1 = keep.tile([P, G, 2 * width], U8, name="x_codes%d" % i, align_bytes=64)
+            t2 = keep.tile([P, G, width], U8, name="x_planes%d" % i, align_bytes=64)
+            x_codes.append(t1)
+            x_planes.append(t2)
+        for i, (c0, width) in enumerate(W_CHUNKS):
+            t1 = keep.tile([P, G, 2 * width], U8, name="w_codes%d" % i, align_bytes=64)
+            t2 = keep.tile([P, G, width], U8, name="w_planes%d" % i, align_bytes=64)
+            w_codes.append(t1)
+            w_planes.append(t2)
+
+        def zero(engine, plane):
+            engine.memset(plane[:].rearrange("p g c -> p (g c)").bitcast(I32), 0)
+
+        def load_codes(dst, src, c0, width):
+            nc.sync.dma_start(
+                out=dst[:].bitcast(I32),
+                in_=src[:, :, 2 * c0 : 2 * (c0 + width)].rearrange("g p c -> p g c").bitcast(I32),
+            )
+
+        def load_planes(dst, src, c0, width):
+            for q in range(4):
+                nc.sync.dma_start(
+                    out=dst[32 * q : 32 * q + 4, :, :].bitcast(I32),
+                    in_=src[:, 4 * q : 4 * q + 4, c0 : c0 + width].rearrange("g r c -> r g c").bitcast(I32),
+                )
+
+        b_nat = keep.tile([P, P], BF16)
+        b_rot = keep.tile([P, 2 * P], BF16)
+        nc.gpsimd.memset(b_nat[:], 0.0)
+        nc.gpsimd.memset(b_rot[:], 0.0)
+        nc.gpsimd.dma_start(out=b_nat[0:48, :], in_=bqkv.rearrange("(t k) -> t k", k=P))
+        nc.gpsimd.dma_start(out=b_rot[0:16, :], in_=bqkv[0 : 2 * E].rearrange("(t k) -> t k", k=2 * P))
+        ident = keep.tile([P, P], F32)
+        make_identity(nc, ident[:])
+
+        zero(nc.vector, x_planes[0])
+        zero(nc.vector, w_planes[0])
+        zero(nc.vector, w_planes[1])
+        for i in (2, 3, 4):
+            zero(nc.gpsimd, w_planes[i])
+        zero(nc.gpsimd, w_planes[5])
+        zero(nc.gpsimd, w_planes[6])
+        zero(nc.gpsimd, x_planes[1])
+
+        load_codes(x_codes[0], x_words, *X_CHUNKS[0])
+        load_codes(w_codes[0], Wqkv_words, *W_CHUNKS[0])
+        load_planes(x_planes[0], x_scales, *X_CHUNKS[0])
+        load_planes(w_planes[0], Wqkv_scales, *W_CHUNKS[0])
+        for i in range(1, len(W_CHUNKS)):
+            load_codes(w_codes[i], Wqkv_words, *W_CHUNKS[i])
+            load_planes(w_planes[i], Wqkv_scales, *W_CHUNKS[i])
+        load_codes(x_codes[1], x_words, *X_CHUNKS[1])
+        load_planes(x_planes[1], x_scales, *X_CHUNKS[1])
+
+        table = keep.tile([P, BANKS, 2, NT], F32)
+        scratch = prod.tile([P, BANKS * 2 * NT], F32, name="products")
+        turns = scratch[:, 0:HALF]
+        cturns = scratch[:, HALF : 2 * HALF]
+        sines = scratch[:, 2 * HALF : 3 * HALF].rearrange("p (r m) -> p r m", r=2)
+        whole = scratch[:, 3 * HALF : 3 * HALF + REDUCED].bitcast(I32)
+
+        warm = small.tile([P, 1], F32)
+        nc.vector.memset(warm[:], 0.0)
+        nc.scalar.activation(out=warm[:], in_=warm[:], func=ACT.Sin)
+
+        one = small.tile([P, 1], F32)
+        nc.vector.memset(one[:], 1.0)
+        nc.vector.tensor_scalar_mul(turns[:, 0:1], one[:], SEQ / (2.0 * math.pi))
+        n = 1
+        while n < HALF:
+            nc.vector.tensor_scalar_mul(turns[:, n : 2 * n], turns[:, 0:n], TURN_RATIO**n)
+            n = 2 * n
+        doubled = keep.tile([P, P], F32)
+        nc.vector.tensor_copy(
+            out=doubled[:].rearrange("p (m e) -> p m e", e=2),
+            in_=turns[:, 0:64].unsqueeze(2).to_broadcast([P, 64, 2]),
+        )
+        nc.vector.tensor_scalar_add(cturns, turns, 0.25)
+        nc.vector.tensor_copy(out=whole, in_=turns[:, 0:REDUCED])
+        nc.vector.tensor_tensor(out=turns[:, 0:REDUCED], in0=turns[:, 0:REDUCED], in1=whole, op=SUB)
+        nc.vector.tensor_copy(out=whole, in_=cturns[:, 0:REDUCED])
+        nc.vector.tensor_tensor(out=cturns[:, 0:REDUCED], in0=cturns[:, 0:REDUCED], in1=whole, op=SUB)
+        nc.scalar.activation(out=sines[:, 0, :], in_=turns[:, 512:1024], func=ACT.Sin, scale=2.0 * math.pi)
+        nc.scalar.activation(out=sines[:, 1, :], in_=turns[:, 0:512], func=ACT.Sin, scale=-2.0 * math.pi)
+        for b in range(BANKS):
+            nc.scalar.activation(
+                out=table[:, b, 0, :].rearrange("p (m e) -> p m e", e=2),
+                in_=cturns[:, 256 * b : 256 * b + 256].unsqueeze(2).to_broadcast([P, 256, 2]),
+                func=ACT.Sin,
+                scale=2.0 * math.pi,
+            )
+        for b in range(BANKS):
+            nc.vector.tensor_copy(
+                out=table[:, b, 1, :].rearrange("p (q h r) -> p q h r", h=2, r=2),
+                in_=sines[:, :, 128 * b : 128 * b + 128].rearrange("p r q -> p q r").unsqueeze(2).to_broadcast([P, 128, 2, 2]),
+            )
+
+        b_nat32 = keep.tile([P, P], F32)
+        b_rot32 = keep.tile([P, 2 * P], F32)
+        nc.scalar.copy(out=b_nat32[:], in_=b_nat[:])
+        nc.scalar.copy(out=b_rot32[:], in_=b_rot[:])
+        flipped = fixed.tile([P, NT], F32, name="fixed3")
+        nc.tensor.transpose(flipped[:, 0:128], doubled[:], ident[:])
+        nc.tensor.transpose(flipped[:, 128:256], b_nat32[:], ident[:])
+        nc.tensor.transpose(flipped[:, 256:384], b_rot32[:, 1 : 2 * P : 2], ident[:])
+        nc.tensor.transpose(flipped[:, 384:512], b_rot32[:, 0 : 2 * P : 2], ident[:])
+        b_cols = keep.tile([P, 48], F32)
+        br_cols = keep.tile([P, 2, 16], F32)
+        angle = keep.tile([P, 2, 16], F32)
+        nc.vector.tensor_copy(out=angle[:, 0, 0:1], in_=flipped[:, 0:1])
+        nc.scalar.copy(out=b_cols[:], in_=flipped[:, 128:176])
+        nc.scalar.copy(out=br_cols[:, :, 0:8], in_=flipped[:, 256:272].rearrange("p (s t) -> p s t", s=2))
+        nc.scalar.copy(out=br_cols[:, :, 8:16], in_=flipped[:, 384:400].rearrange("p (s t) -> p s t", s=2))
+        n = 1
+        while n < 16:
+            nc.vector.tensor_scalar_mul(angle[:, 0, n : 2 * n], angle[:, 0, 0:n], TURN_RATIO ** (64 * n))
+            n = 2 * n
+        nc.vector.tensor_scalar_add(angle[:, 1, :], angle[:, 0, :], 0.25)
+        angle_whole = keep.tile([P, 2, 16], I32)
+        nc.vector.tensor_copy(out=angle_whole[:], in_=angle[:])
+        nc.vector.tensor_tensor(out=angle[:], in0=angle[:], in1=angle_whole[:], op=SUB)
+        trig = keep.tile([P, 2, 16], F32)
+        nc.scalar.activation(out=trig[:, 0, 0:8], in_=angle[:, 0, 0:8], func=ACT.Sin, scale=-2.0 * math.pi)
+        nc.scalar.activation(out=trig[:, 0, 8:16], in_=angle[:, 0, 8:16], func=ACT.Sin, scale=2.0 * math.pi)
+        nc.scalar.activation(out=trig[:, 1, :], in_=angle[:, 1, :], func=ACT.Sin, scale=2.0 * math.pi)
+        mixed = keep.tile([P, 2, 16], F32)
+        mixed_b = keep.tile([P, 2, 16], F32)
+        bias_hi = keep.tile([P, 2, HALF], F32)
+        bias_v = keep.tile([P, E], F32)
+        bias_lo = {}
+
+        def mixed_columns():
+            nc.vector.tensor_tensor(
+                out=mixed[:], in0=b_cols[:, 0:32].rearrange("p (s t) -> p s t", s=2),
+                in1=trig[:, 1, :].unsqueeze(1).to_broadcast([P, 2, 16]), op=MULT,
+            )
+            nc.vector.tensor_tensor(
+                out=mixed_b[:], in0=br_cols[:], in1=trig[:, 0, :].unsqueeze(1).to_broadcast([P, 2, 16]), op=MULT
+            )
+            nc.vector.tensor_tensor(out=mixed[:], in0=mixed[:], in1=mixed_b[:], op=ADD)
+
+        def spread(bank, cols, t0):
+            for t in range(4):
+                nc.tensor.transpose(
+                    bank[:, 128 * t : 128 * t + 128], cols[:, t0 + t : t0 + t + 1].to_broadcast([P, P]), ident[:]
+                )
+
+        def spread_mixed():
+            for s in range(2):
+                for b in range(2):
+                    bank = fixed.tile([P, NT], F32, name="fixed%d" % (2 * s + b))
+                    spread(bank, mixed[:, s, :], 4 * b)
+                    bias_lo[s, b] = bank
+            for s in range(2):
+                for b in range(2):
+                    bank = acc.tile([P, NT], F32, name="bank")
+                    spread(bank, mixed[:, s, :], 8 + 4 * b)
+                    nc.scalar.copy(out=bias_hi[:, s, NT * b : NT * b + NT], in_=bank[:])
+
+        def spread_v():
+            for b in range(4):
+                bank = acc.tile([P, NT], F32, name="bank")
+                spread(bank, b_cols[:], 32 + 4 * b)
+                nc.scalar.copy(out=bias_v[:, NT * b : NT * b + NT], in_=bank[:])
+
+        def matmuls(tile, col):
+            xi = 0 if P * tile < X_CHUNKS[1][0] else 1
+            xo = P * tile - X_CHUNKS[xi][0]
+            wi = [i for i, (c0, width) in enumerate(W_CHUNKS) if c0 <= col < c0 + width][0]
+            wo = col - W_CHUNKS[wi][0]
+            bank = acc.tile([P, NT], F32, name="bank")
+            for g in range(G):
+                nc.tensor.matmul_mx(
+                    out=bank[:],
+                    lhsT=x_codes[xi][:, g, 2 * xo : 2 * xo + 2 * P].bitcast(FP4X4),
+                    lhsT_scale=x_planes[xi][:, g, xo : xo + P],
+                    rhs=w_codes[wi][:, g, 2 * wo : 2 * wo + 2 * NT].bitcast(FP4X4),
+                    rhs_scale=w_planes[wi][:, g, wo : wo + NT],
+                    start=(g == 0),
+                    stop=(g == G - 1),
+                )
+            return bank
+
+        def product(pr, tile, s, b):
+            bank = matmuls(tile, E * s + NT * b)
+            nc.vector.tensor_tensor(
+                out=pr[:, b, :, :], in0=bank[:].unsqueeze(1).to_broadcast([P, 2, NT]), in1=table[:, b, :, :], op=MULT
+            )
+
+        def add_low_bias(pr, s, b):
+            nc.vector.tensor_tensor(out=pr[:, b, 0, :], in0=pr[:, b, 0, :], in1=bias_lo[s, b][:], op=ADD)
+
+        def parts(pr, half):
+            a = pr[:, 2 * half : 2 * half + 2, 0, :].rearrange("p b (h k) -> p b h k", h=2)
+            r = pr[:, :, 1, 1 - half : NT : 2].rearrange("p (b h) k -> p b h k", h=2)
+            return a, r
+
+        def add_halves(engine, pr, z, half):
+            a, r = parts(pr, half)
+            engine.tensor_tensor(
+                out=z[:, HALF * half : HALF * half + HALF].rearrange("p (b h k) -> p b h k", b=2, h=2), in0=a, in1=r, op=ADD
+            )
+
+        def finish(pr, tile, s):
+            z = zs.tile([P, E], F32, name="z")
+            add_halves(nc.gpsimd, pr, z, 1)
+            add_halves(nc.gpsimd, pr, z, 0)
+            nc.gpsimd.tensor_tensor(out=z[:, HALF:E], in0=z[:, HALF:E], in1=bias_hi[:, s, :], op=ADD)
+            norm(z, tile, s)
+
+        def norm(z, tile, s):
+            squares = junk.tile([P, E], BF16, name="squares")
+            total = small.tile([P, 1], F32, name="total")
+            factor = small.tile([P, 1], F32, name="factor")
+            nc.scalar.activation(out=squares[:], in_=z[:], func=ACT.Square, accum_out=total[:])
+            nc.scalar.activation(out=factor[:], in_=total[:], func=ACT.Relu, bias=-1e-24)
+            nc.scalar.activation(out=factor[:], in_=factor[:], func=ACT.Abs_reciprocal_sqrt, bias=1e-24)
+            nc.scalar.activation(out=z[:], in_=z[:], func=ACT.Copy, scale=factor[:])
+            nc.sync.dma_start(out=outs[s][P * tile : P * tile + P, :], in_=z[:])
+
+        v_tiles = {}
+
+        def value(tile, b):
+            if b == 0:
+                vt = vs.tile([P, E], F32, name="v_out")
+                v_tiles[tile] = vt
+            vt = v_tiles[tile]
+            bank = matmuls(tile, 2 * E + NT * b)
+            nc.vector.tensor_tensor(
+                out=vt[:, NT * b : NT * b + NT], in0=bank[:], in1=bias_v[:, NT * b : NT * b + NT], op=ADD
+            )
+            if tile == TILES - 1:
+                nc.sync.dma_start(
+                    out=outs[2][P * tile : P * tile + P, NT * b : NT * b + NT], in_=vt[:, NT * b : NT * b + NT]
+                )
+            elif b == 3:
+                nc.sync.dma_start(out=outs[2][P * tile : P * tile + P, :], in_=vt[:])
+
+        first = prod.tile([P, BANKS, 2, NT], F32, name="products")
+        for b in range(4):
+            product(first, 0, 0, b)
+        mixed_columns()
+        spread_mixed()
+        second = prod.tile([P, BANKS, 2, NT], F32, name="products")
+        for b in range(4):
+            product(second, 1, 0, b)
+        spread_v()
+        early = []
+        for t, pr in ((0, first), (1, second)):
+            z = zs.tile([P, E], F32, name="z")
+            add_halves(nc.gpsimd, pr, z, 1)
+            add_halves(nc.gpsimd, pr, z, 0)
+            nc.gpsimd.tensor_tensor(out=z[:, HALF:E], in0=z[:, HALF:E], in1=bias_hi[:, 0, :], op=ADD)
+            early.append(z)
+
+        units = [(0, 1), (1, 1)] + [(t, s) for t in range(2, TILES) for s in range(2)]
+        values = {u: [] for u in units}
+        for t in (0, 1):
+            values[t, 1] = [(t, b) for b in range(4)]
+        for t in range(2, TILES - 1):
+            values[t, 0] = [(t, 0), (t, 1)]
+            values[t, 1] = [(t, 2), (t, 3)]
+        for t, s in units:
+            pr = prod.tile([P, BANKS, 2, NT], F32, name="products")
+            mine = values[t, s]
+            product(pr, t, s, 0)
+            product(pr, t, s, 1)
+            for tv, b in mine[0:1]:
+                value(tv, b)
+            add_low_bias(pr, s, 0)
+            product(pr, t, s, 2)
+            add_low_bias(pr, s, 1)
+            product(pr, t, s, 3)
+            if early:
+                z = early.pop(0)
+                for b in range(2):
+                    lo = z[:, NT * b : NT * b + NT]
+                    nc.vector.tensor_tensor(out=lo, in0=lo, in1=bias_lo[0, b][:], op=ADD)
+                norm(z, t, 0)
+            for tv, b in mine[1:]:
+                value(tv, b)
+            if (t, s) != (TILES - 1, 1):
+                finish(pr, t, s)
+        z = zs.tile([P, E], F32, name="z")
+        add_halves(nc.vector, pr, z, 0)
+        add_halves(nc.vector, pr, z, 1)
+        value(TILES - 1, 0)
+        nc.vector.tensor_tensor(out=z[:, HALF:E], in0=z[:, HALF:E], in1=bias_hi[:, 1, :], op=ADD)
+        for b in range(1, 4):
+            value(TILES - 1, b)
+        squares = junk.tile([P, E], BF16, name="squares")
+        sums = small.tile([P, 2], F32, name="sums")
+        factor = small.tile([P, 1], F32, name="factor")
+        for h in range(2):
+            cols = slice(HALF * h, HALF * h + HALF)
+            nc.scalar.activation(out=squares[:, cols], in_=z[:, cols], func=ACT.Square, accum_out=sums[:, h : h + 1])
+        nc.scalar.activation(out=factor[:], in_=sums[:, 0:1], func=ACT.Identity, bias=sums[:, 1:2])
+        nc.scalar.activation(out=factor[:], in_=factor[:], func=ACT.Relu, bias=-1e-24)
+        nc.scalar.activation(out=factor[:], in_=factor[:], func=ACT.Abs_reciprocal_sqrt, bias=1e-24)
+        nc.scalar.activation(out=z[:, 0:HALF], in_=z[:, 0:HALF], func=ACT.Copy, scale=factor[:])
+        nc.vector.tensor_scalar_mul(z[:, HALF:E], z[:, HALF:E], factor[:])
+        rows = slice(P * (TILES - 1), P * TILES)
+        nc.sync.dma_start(out=outs[1][rows, HALF:E], in_=z[:, HALF:E])
+        nc.sync.dma_start(out=outs[1][rows, 0:HALF], in_=z[:, 0:HALF])

@@ -238,7 +238,7 @@ def tile_multiheadattention_pa_kernel(tc, x_words, x_scales, Wqkv_words, Wqkv_sc
             )
 
         def add_low_bias(pr, s, b):
-            nc.vector.tensor_tensor(out=pr[:, b, 0, :], in0=pr[:, b, 0, :], in1=bias_lo[s, b][:], op=ADD)
+            nc.vector.tensor_tensor(out=pr[:, b, 0, :], in0=bias_lo[s, b][:], in1=pr[:, b, 0, :], op=ADD)
 
         def parts(pr, half):
             a = pr[:, 2 * half : 2 * half + 2, 0, :].rearrange("p b (h k) -> p b h k", h=2)
@@ -286,58 +286,61 @@ def tile_multiheadattention_pa_kernel(tc, x_words, x_scales, Wqkv_words, Wqkv_sc
             elif b == 3:
                 nc.sync.dma_start(out=outs[2][P * tile : P * tile + P, :], in_=vt[:])
 
-        first = prod.tile([P, BANKS, 2, NT], F32, name="products")
-        for b in range(4):
-            product(first, 0, 0, b)
-        mixed_columns()
-        spread_mixed()
-        second = prod.tile([P, BANKS, 2, NT], F32, name="products")
-        for b in range(4):
-            product(second, 1, 0, b)
-        spread_v()
+        units = [(0, 0), (1, 0), (0, 1), (1, 1)] + [(t, s) for t in range(2, TILES) for s in range(2)]
+        v_queue = [(t, b) for t in range(TILES) for b in range(4)]
+        V_FIRST = 4
+        V_LEFT = 4
+        done_v = 0
         early = []
-        for t, pr in ((0, first), (1, second)):
-            z = zs.tile([P, E], F32, name="z")
-            add_halves(nc.gpsimd, pr, z, 1)
-            add_halves(nc.gpsimd, pr, z, 0)
-            nc.gpsimd.tensor_tensor(out=z[:, HALF:E], in0=z[:, HALF:E], in1=bias_hi[:, 0, :], op=ADD)
-            early.append(z)
-
-        units = [(0, 1), (1, 1)] + [(t, s) for t in range(2, TILES) for s in range(2)]
-        values = {u: [] for u in units}
-        for t in (0, 1):
-            values[t, 1] = [(t, b) for b in range(4)]
-        for t in range(2, TILES - 1):
-            values[t, 0] = [(t, 0), (t, 1)]
-            values[t, 1] = [(t, 2), (t, 3)]
-        for t, s in units:
+        for n, (t, s) in enumerate(units):
             pr = prod.tile([P, BANKS, 2, NT], F32, name="products")
-            mine = values[t, s]
+            want = 0 if n < V_FIRST else ((n + 1 - V_FIRST) * (len(v_queue) - V_LEFT)) // (len(units) - V_FIRST)
             product(pr, t, s, 0)
             product(pr, t, s, 1)
-            for tv, b in mine[0:1]:
-                value(tv, b)
-            add_low_bias(pr, s, 0)
+            if done_v < want:
+                value(*v_queue[done_v])
+                done_v += 1
+            if n >= 2:
+                add_low_bias(pr, s, 0)
             product(pr, t, s, 2)
-            add_low_bias(pr, s, 1)
+            if n >= 2:
+                add_low_bias(pr, s, 1)
             product(pr, t, s, 3)
-            if early:
-                z = early.pop(0)
+            if n == 0:
+                mixed_columns()
+                spread_mixed()
+            if n == 2:
+                spread_v()
+            while done_v < want:
+                value(*v_queue[done_v])
+                done_v += 1
+            if n < 2:
+                z = zs.tile([P, E], F32, name="z")
+                add_halves(nc.gpsimd, pr, z, 1)
+                add_halves(nc.gpsimd, pr, z, 0)
+                nc.gpsimd.tensor_tensor(out=z[:, HALF:E], in0=z[:, HALF:E], in1=bias_hi[:, 0, :], op=ADD)
+                early.append((z, t, s))
+            elif n < len(units) - 2:
+                finish(pr, t, s)
+            else:
+                z = zs.tile([P, E], F32, name="z")
+                add_halves(nc.vector, pr, z, 0)
+                add_halves(nc.vector, pr, z, 1)
+                value(*v_queue[done_v])
+                done_v += 1
+                nc.vector.tensor_tensor(out=z[:, HALF:E], in0=z[:, HALF:E], in1=bias_hi[:, s, :], op=ADD)
+                if s == 0:
+                    norm(z, t, s)
+            if n in (2, 3):
+                z, te, se = early.pop(0)
                 for b in range(2):
                     lo = z[:, NT * b : NT * b + NT]
-                    nc.vector.tensor_tensor(out=lo, in0=lo, in1=bias_lo[0, b][:], op=ADD)
-                norm(z, t, 0)
-            for tv, b in mine[1:]:
-                value(tv, b)
-            if (t, s) != (TILES - 1, 1):
-                finish(pr, t, s)
-        z = zs.tile([P, E], F32, name="z")
-        add_halves(nc.vector, pr, z, 0)
-        add_halves(nc.vector, pr, z, 1)
-        value(TILES - 1, 0)
-        nc.vector.tensor_tensor(out=z[:, HALF:E], in0=z[:, HALF:E], in1=bias_hi[:, 1, :], op=ADD)
-        for b in range(1, 4):
-            value(TILES - 1, b)
+                    nc.vector.tensor_tensor(out=lo, in0=bias_lo[se, b][:], in1=lo, op=ADD)
+                norm(z, te, se)
+
+        while done_v < len(v_queue):
+            value(*v_queue[done_v])
+            done_v += 1
         squares = junk.tile([P, E], BF16, name="squares")
         sums = small.tile([P, 2], F32, name="sums")
         factor = small.tile([P, 1], F32, name="factor")

@@ -102,12 +102,12 @@ def tile_multiheadattention_pa_kernel(tc, x_words, x_scales, Wqkv_words, Wqkv_sc
         load_codes(x_codes[1], x_words, *X_CHUNKS[1])
         load_planes(x_planes[1], x_scales, *X_CHUNKS[1])
 
-        table = keep.tile([P, BANKS, 2, NT], F32)
+        cosines = keep.tile([P, E], F32)
+        sines = keep.tile([P, BANKS, 2, NT // 2], F32)
         scratch = prod.tile([P, BANKS * 2 * NT], F32, name="products")
         turns = scratch[:, 0:HALF]
         cturns = scratch[:, HALF : 2 * HALF]
-        sines = scratch[:, 2 * HALF : 3 * HALF].rearrange("p (r m) -> p r m", r=2)
-        whole = scratch[:, 3 * HALF : 3 * HALF + REDUCED].bitcast(I32)
+        whole = scratch[:, 2 * HALF : 2 * HALF + REDUCED].bitcast(I32)
 
         warm = small.tile([P, 1], F32)
         nc.vector.memset(warm[:], 0.0)
@@ -130,19 +130,20 @@ def tile_multiheadattention_pa_kernel(tc, x_words, x_scales, Wqkv_words, Wqkv_sc
         nc.vector.tensor_tensor(out=turns[:, 0:REDUCED], in0=turns[:, 0:REDUCED], in1=whole, op=SUB)
         nc.vector.tensor_copy(out=whole, in_=cturns[:, 0:REDUCED])
         nc.vector.tensor_tensor(out=cturns[:, 0:REDUCED], in0=cturns[:, 0:REDUCED], in1=whole, op=SUB)
-        nc.scalar.activation(out=sines[:, 0, :], in_=turns[:, 512:1024], func=ACT.Sin, scale=2.0 * math.pi)
-        nc.scalar.activation(out=sines[:, 1, :], in_=turns[:, 0:512], func=ACT.Sin, scale=-2.0 * math.pi)
-        for b in range(BANKS):
+        for r, sign in ((0, 1.0), (1, -1.0)):
+            m0 = NT * (1 - r)
             nc.scalar.activation(
-                out=table[:, b, 0, :].rearrange("p (m e) -> p m e", e=2),
-                in_=cturns[:, 256 * b : 256 * b + 256].unsqueeze(2).to_broadcast([P, 256, 2]),
+                out=sines[:, :, r, :].rearrange("p b (q e) -> p b q e", e=2),
+                in_=turns[:, m0 : m0 + NT].rearrange("p (b q) -> p b q", b=BANKS).unsqueeze(3).to_broadcast([P, BANKS, P, 2]),
+                func=ACT.Sin,
+                scale=sign * 2.0 * math.pi,
+            )
+        for h in range(2):
+            nc.scalar.activation(
+                out=cosines[:, HALF * h : HALF * h + HALF].rearrange("p (m e) -> p m e", e=2),
+                in_=cturns[:, NT * h : NT * h + NT].unsqueeze(2).to_broadcast([P, NT, 2]),
                 func=ACT.Sin,
                 scale=2.0 * math.pi,
-            )
-        for b in range(BANKS):
-            nc.vector.tensor_copy(
-                out=table[:, b, 1, :].rearrange("p (q h r) -> p q h r", h=2, r=2),
-                in_=sines[:, :, 128 * b : 128 * b + 128].rearrange("p r q -> p q r").unsqueeze(2).to_broadcast([P, 128, 2, 2]),
             )
 
         b_nat32 = keep.tile([P, P], F32)
@@ -231,31 +232,43 @@ def tile_multiheadattention_pa_kernel(tc, x_words, x_scales, Wqkv_words, Wqkv_sc
                 )
             return bank
 
+        def place(b):
+            return NT * ((b + 2) % BANKS)
+
         def product(pr, tile, s, b):
             bank = matmuls(tile, E * s + NT * b)
             nc.vector.tensor_tensor(
-                out=pr[:, b, :, :], in0=bank[:].unsqueeze(1).to_broadcast([P, 2, NT]), in1=table[:, b, :, :], op=MULT
+                out=pr[:, 1, NT * b : NT * b + NT].rearrange("p (r k) -> p r k", r=2),
+                in0=bank[:].rearrange("p (k r) -> p r k", r=2), in1=sines[:, b, :, :], op=MULT,
+            )
+            nc.vector.tensor_tensor(
+                out=pr[:, 0, place(b) : place(b) + NT], in0=bank[:], in1=cosines[:, NT * b : NT * b + NT], op=MULT
             )
 
         def add_low_bias(pr, s, b):
-            nc.vector.tensor_tensor(out=pr[:, b, 0, :], in0=bias_lo[s, b][:], in1=pr[:, b, 0, :], op=ADD)
+            a = pr[:, 0, place(b) : place(b) + NT]
+            nc.vector.tensor_tensor(out=a, in0=bias_lo[s, b][:], in1=a, op=ADD)
 
-        def parts(pr, half):
-            a = pr[:, 2 * half : 2 * half + 2, 0, :].rearrange("p b (h k) -> p b h k", h=2)
-            r = pr[:, :, 1, 1 - half : NT : 2].rearrange("p (b h) k -> p b h k", h=2)
-            return a, r
-
-        def add_halves(engine, pr, z, half):
-            a, r = parts(pr, half)
+        def add_terms(engine, pr, z):
             engine.tensor_tensor(
-                out=z[:, HALF * half : HALF * half + HALF].rearrange("p (b h k) -> p b h k", b=2, h=2), in0=a, in1=r, op=ADD
+                out=z[:].rearrange("p (r b k) -> p r b k", r=2, b=BANKS),
+                in0=pr[:, 0, :].rearrange("p (r b k) -> p r b k", r=2, b=BANKS),
+                in1=pr[:, 1, :].rearrange("p (b r k) -> p r b k", b=BANKS, r=2),
+                op=ADD,
             )
+
+        def add_high_bias(engine, z, s):
+            engine.tensor_tensor(out=z[:, 0:HALF], in0=z[:, 0:HALF], in1=bias_hi[:, s, :], op=ADD)
+
+        def store(z, tile, s):
+            rows = slice(P * tile, P * tile + P)
+            nc.sync.dma_start(out=outs[s][rows, HALF:E], in_=z[:, 0:HALF])
+            nc.sync.dma_start(out=outs[s][rows, 0:HALF], in_=z[:, HALF:E])
 
         def finish(pr, tile, s):
             z = zs.tile([P, E], F32, name="z")
-            add_halves(nc.gpsimd, pr, z, 1)
-            add_halves(nc.gpsimd, pr, z, 0)
-            nc.gpsimd.tensor_tensor(out=z[:, HALF:E], in0=z[:, HALF:E], in1=bias_hi[:, s, :], op=ADD)
+            add_terms(nc.gpsimd, pr, z)
+            add_high_bias(nc.gpsimd, z, s)
             norm(z, tile, s)
 
         def norm(z, tile, s):
@@ -266,7 +279,7 @@ def tile_multiheadattention_pa_kernel(tc, x_words, x_scales, Wqkv_words, Wqkv_sc
             nc.scalar.activation(out=factor[:], in_=total[:], func=ACT.Relu, bias=-1e-24)
             nc.scalar.activation(out=factor[:], in_=factor[:], func=ACT.Abs_reciprocal_sqrt, bias=1e-24)
             nc.scalar.activation(out=z[:], in_=z[:], func=ACT.Copy, scale=factor[:])
-            nc.sync.dma_start(out=outs[s][P * tile : P * tile + P, :], in_=z[:])
+            store(z, tile, s)
 
         v_tiles = {}
 
@@ -293,7 +306,7 @@ def tile_multiheadattention_pa_kernel(tc, x_words, x_scales, Wqkv_words, Wqkv_sc
         done_v = 0
         early = []
         for n, (t, s) in enumerate(units):
-            pr = prod.tile([P, BANKS, 2, NT], F32, name="products")
+            pr = prod.tile([P, 2, E], F32, name="products")
             want = 0 if n < V_FIRST else ((n + 1 - V_FIRST) * (len(v_queue) - V_LEFT)) // (len(units) - V_FIRST)
             product(pr, t, s, 0)
             product(pr, t, s, 1)
@@ -316,25 +329,23 @@ def tile_multiheadattention_pa_kernel(tc, x_words, x_scales, Wqkv_words, Wqkv_sc
                 done_v += 1
             if n < 2:
                 z = zs.tile([P, E], F32, name="z")
-                add_halves(nc.gpsimd, pr, z, 1)
-                add_halves(nc.gpsimd, pr, z, 0)
-                nc.gpsimd.tensor_tensor(out=z[:, HALF:E], in0=z[:, HALF:E], in1=bias_hi[:, 0, :], op=ADD)
+                add_terms(nc.gpsimd, pr, z)
+                add_high_bias(nc.gpsimd, z, s)
                 early.append((z, t, s))
             elif n < len(units) - 2:
                 finish(pr, t, s)
             else:
                 z = zs.tile([P, E], F32, name="z")
-                add_halves(nc.vector, pr, z, 0)
-                add_halves(nc.vector, pr, z, 1)
+                add_terms(nc.vector, pr, z)
                 value(*v_queue[done_v])
                 done_v += 1
-                nc.vector.tensor_tensor(out=z[:, HALF:E], in0=z[:, HALF:E], in1=bias_hi[:, s, :], op=ADD)
+                add_high_bias(nc.vector, z, s)
                 if s == 0:
                     norm(z, t, s)
             if n in (2, 3):
                 z, te, se = early.pop(0)
                 for b in range(2):
-                    lo = z[:, NT * b : NT * b + NT]
+                    lo = z[:, place(b) : place(b) + NT]
                     nc.vector.tensor_tensor(out=lo, in0=bias_lo[se, b][:], in1=lo, op=ADD)
                 norm(z, te, se)
 
@@ -353,5 +364,5 @@ def tile_multiheadattention_pa_kernel(tc, x_words, x_scales, Wqkv_words, Wqkv_sc
         nc.scalar.activation(out=z[:, 0:HALF], in_=z[:, 0:HALF], func=ACT.Copy, scale=factor[:])
         nc.vector.tensor_scalar_mul(z[:, HALF:E], z[:, HALF:E], factor[:])
         rows = slice(P * (TILES - 1), P * TILES)
-        nc.sync.dma_start(out=outs[1][rows, HALF:E], in_=z[:, HALF:E])
-        nc.sync.dma_start(out=outs[1][rows, 0:HALF], in_=z[:, 0:HALF])
+        nc.sync.dma_start(out=outs[1][rows, 0:HALF], in_=z[:, HALF:E])
+        nc.sync.dma_start(out=outs[1][rows, HALF:E], in_=z[:, 0:HALF])

@@ -23,6 +23,8 @@ NT = 512
 BANKS = E // NT
 TILES = TOK // P
 ROPE_BASE = 10000.0
+VECTOR_UNITS = (23,)
+LOW = [(0, 0), (0, 1), (0, 2), (1, 0), (1, 1)]
 FLOPS = 2 * TOK * E * 3 * E
 
 HALF = E // 2
@@ -39,11 +41,11 @@ def tile_multiheadattention_pa_kernel(tc, x_words, x_scales, Wqkv_words, Wqkv_sc
         keep = ctx.enter_context(tc.tile_pool(name="keep", bufs=1))
         prod = ctx.enter_context(tc.tile_pool(name="prod", bufs=3))
         zs = ctx.enter_context(tc.tile_pool(name="zs", bufs=4))
-        vs = ctx.enter_context(tc.tile_pool(name="vs", bufs=2))
+        vs = ctx.enter_context(tc.tile_pool(name="vs", bufs=3))
         junk = ctx.enter_context(tc.tile_pool(name="junk", bufs=1))
         small = ctx.enter_context(tc.tile_pool(name="small", bufs=4))
         fixed = ctx.enter_context(tc.psum_pool(name="fixed", bufs=1))
-        acc = ctx.enter_context(tc.psum_pool(name="acc", bufs=4))
+        acc = ctx.enter_context(tc.psum_pool(name="acc", bufs=8 - len(LOW)))
         ctx.enter_context(tc.manual_schedule())
 
         x_codes, x_planes, w_codes, w_planes = [], [], [], []
@@ -125,11 +127,24 @@ def tile_multiheadattention_pa_kernel(tc, x_words, x_scales, Wqkv_words, Wqkv_sc
             out=doubled[:].rearrange("p (m e) -> p m e", e=2),
             in_=turns[:, 0:64].unsqueeze(2).to_broadcast([P, 64, 2]),
         )
+        first_column = fixed.tile([P, NT], F32, name="fixed2")
+        nc.tensor.transpose(first_column[:, 0:128], doubled[:], ident[:])
         nc.vector.tensor_scalar_add(cturns, turns, 0.25)
         nc.vector.tensor_copy(out=whole, in_=turns[:, 0:REDUCED])
         nc.vector.tensor_tensor(out=turns[:, 0:REDUCED], in0=turns[:, 0:REDUCED], in1=whole, op=SUB)
         nc.vector.tensor_copy(out=whole, in_=cturns[:, 0:REDUCED])
         nc.vector.tensor_tensor(out=cturns[:, 0:REDUCED], in0=cturns[:, 0:REDUCED], in1=whole, op=SUB)
+        angle = keep.tile([P, 2, 16], F32)
+        angle_whole = keep.tile([P, 2, 16], I32)
+        trig = keep.tile([P, 2, 16], F32)
+        nc.vector.tensor_copy(out=angle[:, 0, 0:1], in_=first_column[:, 0:1])
+        n = 1
+        while n < 16:
+            nc.vector.tensor_scalar_mul(angle[:, 0, n : 2 * n], angle[:, 0, 0:n], TURN_RATIO ** (64 * n))
+            n = 2 * n
+        nc.vector.tensor_scalar_add(angle[:, 1, :], angle[:, 0, :], 0.25)
+        nc.vector.tensor_copy(out=angle_whole[:], in_=angle[:])
+        nc.vector.tensor_tensor(out=angle[:], in0=angle[:], in1=angle_whole[:], op=SUB)
         for r, sign in ((0, 1.0), (1, -1.0)):
             m0 = NT * (1 - r)
             nc.scalar.activation(
@@ -148,47 +163,40 @@ def tile_multiheadattention_pa_kernel(tc, x_words, x_scales, Wqkv_words, Wqkv_sc
 
         b_nat32 = keep.tile([P, P], F32)
         b_rot32 = keep.tile([P, 2 * P], F32)
-        nc.scalar.copy(out=b_nat32[:], in_=b_nat[:])
-        nc.scalar.copy(out=b_rot32[:], in_=b_rot[:])
-        flipped = fixed.tile([P, NT], F32, name="fixed3")
-        nc.tensor.transpose(flipped[:, 0:128], doubled[:], ident[:])
-        nc.tensor.transpose(flipped[:, 128:256], b_nat32[:], ident[:])
-        nc.tensor.transpose(flipped[:, 256:384], b_rot32[:, 1 : 2 * P : 2], ident[:])
-        nc.tensor.transpose(flipped[:, 384:512], b_rot32[:, 0 : 2 * P : 2], ident[:])
-        b_cols = keep.tile([P, 48], F32)
-        br_cols = keep.tile([P, 2, 16], F32)
-        angle = keep.tile([P, 2, 16], F32)
-        nc.vector.tensor_copy(out=angle[:, 0, 0:1], in_=flipped[:, 0:1])
-        nc.scalar.copy(out=b_cols[:], in_=flipped[:, 128:176])
-        nc.scalar.copy(out=br_cols[:, :, 0:8], in_=flipped[:, 256:272].rearrange("p (s t) -> p s t", s=2))
-        nc.scalar.copy(out=br_cols[:, :, 8:16], in_=flipped[:, 384:400].rearrange("p (s t) -> p s t", s=2))
-        n = 1
-        while n < 16:
-            nc.vector.tensor_scalar_mul(angle[:, 0, n : 2 * n], angle[:, 0, 0:n], TURN_RATIO ** (64 * n))
-            n = 2 * n
-        nc.vector.tensor_scalar_add(angle[:, 1, :], angle[:, 0, :], 0.25)
-        angle_whole = keep.tile([P, 2, 16], I32)
-        nc.vector.tensor_copy(out=angle_whole[:], in_=angle[:])
-        nc.vector.tensor_tensor(out=angle[:], in0=angle[:], in1=angle_whole[:], op=SUB)
-        trig = keep.tile([P, 2, 16], F32)
         nc.scalar.activation(out=trig[:, 0, 0:8], in_=angle[:, 0, 0:8], func=ACT.Sin, scale=-2.0 * math.pi)
         nc.scalar.activation(out=trig[:, 0, 8:16], in_=angle[:, 0, 8:16], func=ACT.Sin, scale=2.0 * math.pi)
         nc.scalar.activation(out=trig[:, 1, :], in_=angle[:, 1, :], func=ACT.Sin, scale=2.0 * math.pi)
+        nc.scalar.copy(out=b_nat32[:], in_=b_nat[:])
+        nc.scalar.copy(out=b_rot32[:], in_=b_rot[:])
+        b_cols = keep.tile([P, 48], F32)
         mixed = keep.tile([P, 2, 16], F32)
         mixed_b = keep.tile([P, 2, 16], F32)
         bias_hi = keep.tile([P, 2, HALF], F32)
         bias_v = keep.tile([P, E], F32)
         bias_lo = {}
+        flipped = {}
 
-        def mixed_columns():
+        def flip_bias():
+            bank = fixed.tile([P, NT], F32, name="fixed3")
+            nc.tensor.transpose(bank[:, 0:128], b_nat32[:], ident[:])
+            nc.tensor.transpose(bank[:, 128:256], b_rot32[:, 1 : 2 * P : 2], ident[:])
+            nc.tensor.transpose(bank[:, 256:384], b_rot32[:, 0 : 2 * P : 2], ident[:])
+            flipped[0] = bank
+
+        def mix_columns():
+            bank = flipped[0]
             nc.vector.tensor_tensor(
-                out=mixed[:], in0=b_cols[:, 0:32].rearrange("p (s t) -> p s t", s=2),
+                out=mixed[:], in0=bank[:, 0:32].rearrange("p (s t) -> p s t", s=2),
                 in1=trig[:, 1, :].unsqueeze(1).to_broadcast([P, 2, 16]), op=MULT,
             )
-            nc.vector.tensor_tensor(
-                out=mixed_b[:], in0=br_cols[:], in1=trig[:, 0, :].unsqueeze(1).to_broadcast([P, 2, 16]), op=MULT
-            )
-            nc.vector.tensor_tensor(out=mixed[:], in0=mixed[:], in1=mixed_b[:], op=ADD)
+            for h in range(2):
+                nc.vector.tensor_tensor(
+                    out=mixed_b[:, :, 8 * h : 8 * h + 8],
+                    in0=bank[:, 128 + 128 * h : 144 + 128 * h].rearrange("p (s t) -> p s t", s=2),
+                    in1=trig[:, 0, 8 * h : 8 * h + 8].unsqueeze(1).to_broadcast([P, 2, 8]), op=MULT,
+                )
+            nc.scalar.copy(out=b_cols[:], in_=bank[:, 0:48])
+            nc.gpsimd.tensor_tensor(out=mixed[:], in0=mixed[:], in1=mixed_b[:], op=ADD)
 
         def spread(bank, cols, t0):
             for t in range(4):
@@ -196,23 +204,20 @@ def tile_multiheadattention_pa_kernel(tc, x_words, x_scales, Wqkv_words, Wqkv_sc
                     bank[:, 128 * t : 128 * t + 128], cols[:, t0 + t : t0 + t + 1].to_broadcast([P, P]), ident[:]
                 )
 
-        def spread_mixed():
-            for s in range(2):
-                for b in range(2):
-                    bank = fixed.tile([P, NT], F32, name="fixed%d" % (2 * s + b))
-                    spread(bank, mixed[:, s, :], 4 * b)
-                    bias_lo[s, b] = bank
-            for s in range(2):
-                for b in range(2):
-                    bank = acc.tile([P, NT], F32, name="bank")
-                    spread(bank, mixed[:, s, :], 8 + 4 * b)
-                    nc.scalar.copy(out=bias_hi[:, s, NT * b : NT * b + NT], in_=bank[:])
+        def spread_low(s, b):
+            bank = fixed.tile([P, NT], F32, name="fixed%d" % LOW.index((s, b)))
+            spread(bank, mixed[:, s, :], 4 * b)
+            bias_lo[s, b] = bank
 
-        def spread_v():
-            for b in range(4):
-                bank = acc.tile([P, NT], F32, name="bank")
-                spread(bank, b_cols[:], 32 + 4 * b)
-                nc.scalar.copy(out=bias_v[:, NT * b : NT * b + NT], in_=bank[:])
+        def spread_high(s, b):
+            bank = acc.tile([P, NT], F32, name="bank")
+            spread(bank, mixed[:, s, :], 8 + 4 * b)
+            nc.scalar.copy(out=bias_hi[:, s, NT * b : NT * b + NT], in_=bank[:])
+
+        def spread_v(b):
+            bank = acc.tile([P, NT], F32, name="bank")
+            spread(bank, b_cols[:], 32 + 4 * b)
+            nc.scalar.copy(out=bias_v[:, NT * b : NT * b + NT], in_=bank[:])
 
         def matmuls(tile, col):
             xi = 0 if P * tile < X_CHUNKS[1][0] else 1
@@ -258,18 +263,14 @@ def tile_multiheadattention_pa_kernel(tc, x_words, x_scales, Wqkv_words, Wqkv_sc
             )
 
         def add_high_bias(engine, z, s):
-            engine.tensor_tensor(out=z[:, 0:HALF], in0=z[:, 0:HALF], in1=bias_hi[:, s, :], op=ADD)
+            c0 = NT * len([1 for l in LOW if l[0] == s and l[1] >= 2])
+            if c0 < HALF:
+                engine.tensor_tensor(out=z[:, c0:HALF], in0=z[:, c0:HALF], in1=bias_hi[:, s, c0:HALF], op=ADD)
 
         def store(z, tile, s):
             rows = slice(P * tile, P * tile + P)
             nc.sync.dma_start(out=outs[s][rows, HALF:E], in_=z[:, 0:HALF])
             nc.sync.dma_start(out=outs[s][rows, 0:HALF], in_=z[:, HALF:E])
-
-        def finish(pr, tile, s):
-            z = zs.tile([P, E], F32, name="z")
-            add_terms(nc.gpsimd, pr, z)
-            add_high_bias(nc.gpsimd, z, s)
-            norm(z, tile, s)
 
         def norm(z, tile, s):
             squares = junk.tile([P, E], BF16, name="squares")
@@ -279,9 +280,9 @@ def tile_multiheadattention_pa_kernel(tc, x_words, x_scales, Wqkv_words, Wqkv_sc
             nc.scalar.activation(out=factor[:], in_=total[:], func=ACT.Relu, bias=-1e-24)
             nc.scalar.activation(out=factor[:], in_=factor[:], func=ACT.Abs_reciprocal_sqrt, bias=1e-24)
             nc.scalar.activation(out=z[:], in_=z[:], func=ACT.Copy, scale=factor[:])
-            store(z, tile, s)
 
         v_tiles = {}
+        stores = []
 
         def value(tile, b):
             if b == 0:
@@ -298,60 +299,80 @@ def tile_multiheadattention_pa_kernel(tc, x_words, x_scales, Wqkv_words, Wqkv_sc
                 )
             elif b == 3:
                 nc.sync.dma_start(out=outs[2][P * tile : P * tile + P, :], in_=vt[:])
+            if stores and tile == TILES - 1 and b in (0, 2):
+                ze, te, se, early = stores.pop(0)
+                store(ze, te, se)
 
         units = [(0, 0), (1, 0), (0, 1), (1, 1)] + [(t, s) for t in range(2, TILES) for s in range(2)]
         v_queue = [(t, b) for t in range(TILES) for b in range(4)]
-        V_FIRST = 4
-        V_LEFT = 4
+        hooks = {(0, 1): [flip_bias], (0, 2): [mix_columns]}
+
+        def hook(n, b, f, *args):
+            hooks.setdefault((n, b), []).append(lambda: f(*args))
+
+        spreads = [(spread_high, 0, b) for b in range(2) if (0, b + 2) not in LOW]
+        spreads += [(spread_high, 1, b) for b in range(2) if (1, b + 2) not in LOW]
+        spreads += [(spread_low, s, b) for s, b in LOW if s == 1] + [(spread_low, s, b) for s, b in LOW if s == 0]
+        places = [(1, 2), (1, 3), (2, 0), (2, 1), (2, 2), (2, 3), (3, 0), (3, 1)]
+        for (f, s, b), at in zip(spreads, places):
+            hook(*at, f, s, b)
+        for b in range(4):
+            hook(3, 2 + b // 2, spread_v, b)
         done_v = 0
-        early = []
+        held = []
+        N = len(units)
         for n, (t, s) in enumerate(units):
             pr = prod.tile([P, 2, E], F32, name="products")
-            want = 0 if n < V_FIRST else ((n + 1 - V_FIRST) * (len(v_queue) - V_LEFT)) // (len(units) - V_FIRST)
-            product(pr, t, s, 0)
-            product(pr, t, s, 1)
-            if done_v < want:
-                value(*v_queue[done_v])
-                done_v += 1
-            if n >= 2:
-                add_low_bias(pr, s, 0)
-            product(pr, t, s, 2)
-            if n >= 2:
-                add_low_bias(pr, s, 1)
-            product(pr, t, s, 3)
-            if n == 0:
-                mixed_columns()
-                spread_mixed()
-            if n == 2:
-                spread_v()
+            want = 0 if n < 4 else ((n + 1 - 4) * (len(v_queue) - 4)) // (N - 4)
+            for b in range(4):
+                product(pr, t, s, b)
+                for f in hooks.get((n, b), []):
+                    f()
+                if n >= 3 and (s, b - 1) in LOW:
+                    add_low_bias(pr, s, b - 1)
+                if done_v < want and b in (1, 3):
+                    value(*v_queue[done_v])
+                    done_v += 1
             while done_v < want:
                 value(*v_queue[done_v])
                 done_v += 1
-            if n < 2:
-                z = zs.tile([P, E], F32, name="z")
-                add_terms(nc.gpsimd, pr, z)
-                add_high_bias(nc.gpsimd, z, s)
-                early.append((z, t, s))
-            elif n < len(units) - 2:
-                finish(pr, t, s)
-            else:
-                z = zs.tile([P, E], F32, name="z")
+            z = zs.tile([P, E], F32, name="z")
+            if n in VECTOR_UNITS:
                 add_terms(nc.vector, pr, z)
-                value(*v_queue[done_v])
-                done_v += 1
+                if done_v < len(v_queue) and n >= N - 2:
+                    value(*v_queue[done_v])
+                    done_v += 1
                 add_high_bias(nc.vector, z, s)
-                if s == 0:
+            else:
+                add_terms(nc.gpsimd, pr, z)
+                if n == 0:
+                    held.append((z, t, s))
+                else:
+                    for zh, th, sh in held:
+                        add_high_bias(nc.gpsimd, zh, sh)
+                    add_high_bias(nc.gpsimd, z, s)
+                    held = []
+            if n < 3:
+                stores.append((z, t, s, True))
+            else:
+                if n == 3:
+                    for ze, te, se, early in stores:
+                        for b in [l[1] for l in LOW if l[0] == se]:
+                            lo = ze[:, place(b) : place(b) + NT]
+                            nc.vector.tensor_tensor(out=lo, in0=bias_lo[se, b][:], in1=lo, op=ADD)
+                        norm(ze, te, se)
+                if n < N - 1:
                     norm(z, t, s)
-            if n in (2, 3):
-                z, te, se = early.pop(0)
-                for b in range(2):
-                    lo = z[:, place(b) : place(b) + NT]
-                    nc.vector.tensor_tensor(out=lo, in0=bias_lo[se, b][:], in1=lo, op=ADD)
-                norm(z, te, se)
+                    stores.append((z, t, s, False))
+            while len(stores) > 2 and n > 3:
+                ze, te, se, early = stores.pop(0)
+                store(ze, te, se)
 
         while done_v < len(v_queue):
             value(*v_queue[done_v])
             done_v += 1
+        for ze, te, se, early in stores:
+            store(ze, te, se)
         squares = junk.tile([P, E], BF16, name="squares")
         sums = small.tile([P, 2], F32, name="sums")
         factor = small.tile([P, 1], F32, name="factor")

@@ -78,6 +78,7 @@ def tile_multiheadattention_pa_kernel(tc, x_words, x_scales, Wqkv_words, Wqkv_sc
 
         b_nat = keep.tile([P, P], BF16)
         b_rot = keep.tile([P, 2 * P], BF16)
+        zero(nc.gpsimd, w_planes[1])
         nc.gpsimd.memset(b_nat[:], 0.0)
         nc.gpsimd.memset(b_rot[:], 0.0)
         nc.gpsimd.dma_start(out=b_nat[0:48, :], in_=bqkv.rearrange("(t k) -> t k", k=P))
@@ -87,7 +88,6 @@ def tile_multiheadattention_pa_kernel(tc, x_words, x_scales, Wqkv_words, Wqkv_sc
 
         zero(nc.vector, x_planes[0])
         zero(nc.vector, w_planes[0])
-        zero(nc.vector, w_planes[1])
         for i in (2, 3, 4):
             zero(nc.gpsimd, w_planes[i])
         zero(nc.gpsimd, w_planes[5])
@@ -104,12 +104,12 @@ def tile_multiheadattention_pa_kernel(tc, x_words, x_scales, Wqkv_words, Wqkv_sc
         load_codes(x_codes[1], x_words, *X_CHUNKS[1])
         load_planes(x_planes[1], x_scales, *X_CHUNKS[1])
 
-        cosines = keep.tile([P, E], F32)
-        sines = keep.tile([P, BANKS, 2, NT // 2], F32)
+        table = keep.tile([P, BANKS, 2, NT], F32)
         scratch = prod.tile([P, BANKS * 2 * NT], F32, name="products")
         turns = scratch[:, 0:HALF]
-        cturns = scratch[:, HALF : 2 * HALF]
-        whole = scratch[:, 2 * HALF : 2 * HALF + REDUCED].bitcast(I32)
+        sines = scratch[:, HALF : 2 * HALF].rearrange("p (b r q) -> p b r q", b=BANKS, r=2)
+        sizes = scratch[:, 2 * HALF : 3 * HALF]
+        whole = scratch[:, 3 * HALF : 3 * HALF + REDUCED].bitcast(I32)
 
         warm = small.tile([P, 1], F32)
         nc.vector.memset(warm[:], 0.0)
@@ -129,45 +129,59 @@ def tile_multiheadattention_pa_kernel(tc, x_words, x_scales, Wqkv_words, Wqkv_sc
         )
         first_column = fixed.tile([P, NT], F32, name="fixed2")
         nc.tensor.transpose(first_column[:, 0:128], doubled[:], ident[:])
-        nc.vector.tensor_scalar_add(cturns, turns, 0.25)
         nc.vector.tensor_copy(out=whole, in_=turns[:, 0:REDUCED])
         nc.vector.tensor_tensor(out=turns[:, 0:REDUCED], in0=turns[:, 0:REDUCED], in1=whole, op=SUB)
-        nc.vector.tensor_copy(out=whole, in_=cturns[:, 0:REDUCED])
-        nc.vector.tensor_tensor(out=cturns[:, 0:REDUCED], in0=cturns[:, 0:REDUCED], in1=whole, op=SUB)
-        angle = keep.tile([P, 2, 16], F32)
-        angle_whole = keep.tile([P, 2, 16], I32)
+
+        def sine(out, in_, sign):
+            nc.scalar.activation(out=out, in_=in_, func=ACT.Sin, scale=sign * 2.0 * math.pi)
+
+        def cosine(out, in_):
+            nc.scalar.activation(out=out, in_=in_, func=ACT.Sin, scale=-2.0 * math.pi, bias=0.5 * math.pi)
+
+        def table_bank(b):
+            sine(sines[:, b, 0, :], turns[:, NT + P * b : NT + P * b + P], 1.0)
+            sine(sines[:, b, 1, :], turns[:, P * b : P * b + P], -1.0)
+            size = sizes[:, 256 * b : 256 * b + 256]
+            nc.scalar.activation(out=size, in_=turns[:, 256 * b : 256 * b + 256], func=ACT.Abs)
+            cosine(
+                table[:, b, 0, :].rearrange("p (m e) -> p m e", e=2), size.unsqueeze(2).to_broadcast([P, 256, 2])
+            )
+
+        def widen_sines(b):
+            nc.vector.tensor_copy(
+                out=table[:, b, 1, :].rearrange("p (q h r) -> p q h r", h=2, r=2),
+                in_=sines[:, b, :, :].rearrange("p r q -> p q r").unsqueeze(2).to_broadcast([P, P, 2, 2]),
+            )
+
+        angle = keep.tile([P, 16], F32)
+        angle_whole = keep.tile([P, 16], I32)
+        angle_size = keep.tile([P, 16], F32)
         trig = keep.tile([P, 2, 16], F32)
-        nc.vector.tensor_copy(out=angle[:, 0, 0:1], in_=first_column[:, 0:1])
-        n = 1
-        while n < 16:
-            nc.vector.tensor_scalar_mul(angle[:, 0, n : 2 * n], angle[:, 0, 0:n], TURN_RATIO ** (64 * n))
-            n = 2 * n
-        nc.vector.tensor_scalar_add(angle[:, 1, :], angle[:, 0, :], 0.25)
-        nc.vector.tensor_copy(out=angle_whole[:], in_=angle[:])
-        nc.vector.tensor_tensor(out=angle[:], in0=angle[:], in1=angle_whole[:], op=SUB)
-        for r, sign in ((0, 1.0), (1, -1.0)):
-            m0 = NT * (1 - r)
-            nc.scalar.activation(
-                out=sines[:, :, r, :].rearrange("p b (q e) -> p b q e", e=2),
-                in_=turns[:, m0 : m0 + NT].rearrange("p (b q) -> p b q", b=BANKS).unsqueeze(3).to_broadcast([P, BANKS, P, 2]),
-                func=ACT.Sin,
-                scale=sign * 2.0 * math.pi,
-            )
-        for h in range(2):
-            nc.scalar.activation(
-                out=cosines[:, HALF * h : HALF * h + HALF].rearrange("p (m e) -> p m e", e=2),
-                in_=cturns[:, NT * h : NT * h + NT].unsqueeze(2).to_broadcast([P, NT, 2]),
-                func=ACT.Sin,
-                scale=2.0 * math.pi,
-            )
+
+        def first_angle():
+            nc.vector.tensor_copy(out=angle[:, 0:1], in_=first_column[:, 0:1])
+
+        def more_angles(n):
+            nc.vector.tensor_scalar_mul(angle[:, n : 2 * n], angle[:, 0:n], TURN_RATIO ** (64 * n))
+
+        def reduce_angles():
+            nc.vector.tensor_copy(out=angle_whole[:], in_=angle[:])
+            nc.vector.tensor_tensor(out=angle[:], in0=angle[:], in1=angle_whole[:], op=SUB)
+            sine(trig[:, 0, 0:8], angle[:, 0:8], -1.0)
+            sine(trig[:, 0, 8:16], angle[:, 8:16], 1.0)
+            nc.scalar.activation(out=angle_size[:], in_=angle[:], func=ACT.Abs)
+            cosine(trig[:, 1, :], angle_size[:])
 
         b_nat32 = keep.tile([P, P], F32)
         b_rot32 = keep.tile([P, 2 * P], F32)
-        nc.scalar.activation(out=trig[:, 0, 0:8], in_=angle[:, 0, 0:8], func=ACT.Sin, scale=-2.0 * math.pi)
-        nc.scalar.activation(out=trig[:, 0, 8:16], in_=angle[:, 0, 8:16], func=ACT.Sin, scale=2.0 * math.pi)
-        nc.scalar.activation(out=trig[:, 1, :], in_=angle[:, 1, :], func=ACT.Sin, scale=2.0 * math.pi)
+        table_bank(0)
+        table_bank(1)
         nc.scalar.copy(out=b_nat32[:], in_=b_nat[:])
         nc.scalar.copy(out=b_rot32[:], in_=b_rot[:])
+        table_bank(2)
+        table_bank(3)
+        widen_sines(0)
+        first_angle()
         b_cols = keep.tile([P, 48], F32)
         mixed = keep.tile([P, 2, 16], F32)
         mixed_b = keep.tile([P, 2, 16], F32)
@@ -237,40 +251,34 @@ def tile_multiheadattention_pa_kernel(tc, x_words, x_scales, Wqkv_words, Wqkv_sc
                 )
             return bank
 
-        def place(b):
-            return NT * ((b + 2) % BANKS)
-
         def product(pr, tile, s, b):
             bank = matmuls(tile, E * s + NT * b)
             nc.vector.tensor_tensor(
-                out=pr[:, 1, NT * b : NT * b + NT].rearrange("p (r k) -> p r k", r=2),
-                in0=bank[:].rearrange("p (k r) -> p r k", r=2), in1=sines[:, b, :, :], op=MULT,
-            )
-            nc.vector.tensor_tensor(
-                out=pr[:, 0, place(b) : place(b) + NT], in0=bank[:], in1=cosines[:, NT * b : NT * b + NT], op=MULT
+                out=pr[:, b, :, :], in0=bank[:].unsqueeze(1).to_broadcast([P, 2, NT]), in1=table[:, b, :, :], op=MULT
             )
 
+        def place(b):
+            return NT * b
+
         def add_low_bias(pr, s, b):
-            a = pr[:, 0, place(b) : place(b) + NT]
+            a = pr[:, b, 0, :]
             nc.vector.tensor_tensor(out=a, in0=bias_lo[s, b][:], in1=a, op=ADD)
 
         def add_terms(engine, pr, z):
-            engine.tensor_tensor(
-                out=z[:].rearrange("p (r b k) -> p r b k", r=2, b=BANKS),
-                in0=pr[:, 0, :].rearrange("p (r b k) -> p r b k", r=2, b=BANKS),
-                in1=pr[:, 1, :].rearrange("p (b r k) -> p r b k", b=BANKS, r=2),
-                op=ADD,
-            )
+            for half in (1, 0):
+                engine.tensor_tensor(
+                    out=z[:, HALF * half : HALF * half + HALF].rearrange("p (b h k) -> p b h k", b=2, h=2),
+                    in0=pr[:, 2 * half : 2 * half + 2, 0, :].rearrange("p b (h k) -> p b h k", h=2),
+                    in1=pr[:, :, 1, 1 - half : NT : 2].rearrange("p (b h) k -> p b h k", h=2),
+                    op=ADD,
+                )
 
         def add_high_bias(engine, z, s):
-            c0 = NT * len([1 for l in LOW if l[0] == s and l[1] >= 2])
-            if c0 < HALF:
-                engine.tensor_tensor(out=z[:, c0:HALF], in0=z[:, c0:HALF], in1=bias_hi[:, s, c0:HALF], op=ADD)
+            c0 = NT * len([1 for l in LOW if l[0] == s])
+            engine.tensor_tensor(out=z[:, c0:E], in0=z[:, c0:E], in1=bias_hi[:, s, c0 - HALF : HALF], op=ADD)
 
         def store(z, tile, s):
-            rows = slice(P * tile, P * tile + P)
-            nc.sync.dma_start(out=outs[s][rows, HALF:E], in_=z[:, 0:HALF])
-            nc.sync.dma_start(out=outs[s][rows, 0:HALF], in_=z[:, HALF:E])
+            nc.sync.dma_start(out=outs[s][P * tile : P * tile + P, :], in_=z[:])
 
         def norm(z, tile, s):
             squares = junk.tile([P, E], BF16, name="squares")
@@ -305,7 +313,11 @@ def tile_multiheadattention_pa_kernel(tc, x_words, x_scales, Wqkv_words, Wqkv_sc
 
         units = [(0, 0), (1, 0), (0, 1), (1, 1)] + [(t, s) for t in range(2, TILES) for s in range(2)]
         v_queue = [(t, b) for t in range(TILES) for b in range(4)]
-        hooks = {(0, 1): [flip_bias], (0, 2): [mix_columns]}
+        hooks = {
+            (0, 0): [lambda: more_angles(1), lambda: widen_sines(1), lambda: more_angles(2)],
+            (0, 1): [flip_bias, lambda: more_angles(4), lambda: widen_sines(2), lambda: more_angles(8), reduce_angles],
+            (0, 2): [lambda: widen_sines(3), mix_columns],
+        }
 
         def hook(n, b, f, *args):
             hooks.setdefault((n, b), []).append(lambda: f(*args))
@@ -322,8 +334,8 @@ def tile_multiheadattention_pa_kernel(tc, x_words, x_scales, Wqkv_words, Wqkv_sc
         held = []
         N = len(units)
         for n, (t, s) in enumerate(units):
-            pr = prod.tile([P, 2, E], F32, name="products")
-            want = 0 if n < 4 else ((n + 1 - 4) * (len(v_queue) - 4)) // (N - 4)
+            pr = prod.tile([P, BANKS, 2, NT], F32, name="products")
+            want = 0 if n < 4 else ((n + 1 - 4) * (len(v_queue) - 3)) // (N - 4)
             for b in range(4):
                 product(pr, t, s, b)
                 for f in hooks.get((n, b), []):
@@ -385,5 +397,5 @@ def tile_multiheadattention_pa_kernel(tc, x_words, x_scales, Wqkv_words, Wqkv_sc
         nc.scalar.activation(out=z[:, 0:HALF], in_=z[:, 0:HALF], func=ACT.Copy, scale=factor[:])
         nc.vector.tensor_scalar_mul(z[:, HALF:E], z[:, HALF:E], factor[:])
         rows = slice(P * (TILES - 1), P * TILES)
-        nc.sync.dma_start(out=outs[1][rows, 0:HALF], in_=z[:, HALF:E])
-        nc.sync.dma_start(out=outs[1][rows, HALF:E], in_=z[:, 0:HALF])
+        nc.sync.dma_start(out=outs[1][rows, HALF:E], in_=z[:, HALF:E])
+        nc.sync.dma_start(out=outs[1][rows, 0:HALF], in_=z[:, 0:HALF])

import math
from contextlib import ExitStack

import concourse.mybir as mybir
from concourse.masks import make_identity

F32 = mybir.dt.float32
BF16 = mybir.dt.bfloat16
I32 = mybir.dt.int32
U8 = mybir.dt.uint8
FP4X4 = mybir.dt.float4_e2m1fn_x4
MULT = mybir.AluOpType.mult
ADD = mybir.AluOpType.add
SUB = mybir.AluOpType.subtract
ACT = mybir.ActivationFunctionType

P = 128
TOK = 1536
SEQ = 384
E = 2048
G = 4
NT = 512
BANKS = E // NT
TILES = TOK // P
ROPE_BASE = 10000.0
VECTOR_UNITS = (23,)
LOW = [(0, 0), (0, 1), (0, 2), (1, 0), (1, 1)]
FLOPS = 2 * TOK * E * 3 * E

HALF = E // 2
TURN_RATIO = ROPE_BASE ** (-2.0 / E)
REDUCED = 640
X_CHUNKS = ((0, 256), (256, 1280))
W_CHUNKS = ((0, 512), (512, 512), (1024, 1024), (2048, 1024), (3072, 1024), (4096, 1024), (5120, 1024))


def tile_multiheadattention_pa_kernel(tc, x_words, x_scales, Wqkv_words, Wqkv_scales, bqkv, out_0, out_1, out_2):
    nc = tc.nc
    outs = [o.flatten_outer_dims() for o in (out_0, out_1, out_2)]
    with ExitStack() as ctx:
        keep = ctx.enter_context(tc.tile_pool(name="keep", bufs=1))
        prod = ctx.enter_context(tc.tile_pool(name="prod", bufs=3))
        zs = ctx.enter_context(tc.tile_pool(name="zs", bufs=4))
        vs = ctx.enter_context(tc.tile_pool(name="vs", bufs=3))
        junk = ctx.enter_context(tc.tile_pool(name="junk", bufs=1))
        small = ctx.enter_context(tc.tile_pool(name="small", bufs=4))
        fixed = ctx.enter_context(tc.psum_pool(name="fixed", bufs=1))
        acc = ctx.enter_context(tc.psum_pool(name="acc", bufs=8 - len(LOW)))
        ctx.enter_context(tc.manual_schedule())

        x_codes, x_planes, w_codes, w_planes = [], [], [], []
        for i, (c0, width) in enumerate(X_CHUNKS):
            t1 = keep.tile([P, G, 2 * width], U8, name="x_codes%d" % i, align_bytes=64)
            t2 = keep.tile([P, G, width], U8, name="x_planes%d" % i, align_bytes=64)
            x_codes.append(t1)
            x_planes.append(t2)
        for i, (c0, width) in enumerate(W_CHUNKS):
            t1 = keep.tile([P, G, 2 * width], U8, name="w_codes%d" % i, align_bytes=64)
            t2 = keep.tile([P, G, width], U8, name="w_planes%d" % i, align_bytes=64)
            w_codes.append(t1)
            w_planes.append(t2)

        def zero(engine, plane):
            engine.memset(plane[:].rearrange("p g c -> p (g c)").bitcast(I32), 0)

        def load_codes(dst, src, c0, width):
            nc.sync.dma_start(
                out=dst[:].bitcast(I32),
                in_=src[:, :, 2 * c0 : 2 * (c0 + width)].rearrange("g p c -> p g c").bitcast(I32),
            )

        def load_planes(dst, src, c0, width):
            for q in range(4):
                nc.sync.dma_start(
                    out=dst[32 * q : 32 * q + 4, :, :].bitcast(I32),
                    in_=src[:, 4 * q : 4 * q + 4, c0 : c0 + width].rearrange("g r c -> r g c").bitcast(I32),
                )

        b_nat = keep.tile([P, P], BF16)
        b_rot = keep.tile([P, 2 * P], BF16)
        zero(nc.gpsimd, w_planes[1])
        nc.gpsimd.memset(b_nat[:], 0.0)
        nc.gpsimd.memset(b_rot[:], 0.0)
        nc.gpsimd.dma_start(out=b_nat[0:48, :], in_=bqkv.rearrange("(t k) -> t k", k=P))
        nc.gpsimd.dma_start(out=b_rot[0:16, :], in_=bqkv[0 : 2 * E].rearrange("(t k) -> t k", k=2 * P))
        ident = keep.tile([P, P], F32)
        make_identity(nc, ident[:])

        zero(nc.vector, x_planes[0])
        zero(nc.vector, w_planes[0])
        for i in (2, 3, 4):
            zero(nc.gpsimd, w_planes[i])
        zero(nc.gpsimd, w_planes[5])
        zero(nc.gpsimd, w_planes[6])
        zero(nc.gpsimd, x_planes[1])

        load_codes(x_codes[0], x_words, *X_CHUNKS[0])
        load_codes(w_codes[0], Wqkv_words, *W_CHUNKS[0])
        load_planes(x_planes[0], x_scales, *X_CHUNKS[0])
        load_planes(w_planes[0], Wqkv_scales, *W_CHUNKS[0])
        for i in range(1, len(W_CHUNKS)):
            load_codes(w_codes[i], Wqkv_words, *W_CHUNKS[i])
            load_planes(w_planes[i], Wqkv_scales, *W_CHUNKS[i])
        load_codes(x_codes[1], x_words, *X_CHUNKS[1])
        load_planes(x_planes[1], x_scales, *X_CHUNKS[1])

        table = keep.tile([P, BANKS, 2, NT], F32)
        scratch = prod.tile([P, BANKS * 2 * NT], F32, name="products")
        turns = scratch[:, 0:HALF]
        sines = scratch[:, HALF : 2 * HALF].rearrange("p (b r q) -> p b r q", b=BANKS, r=2)
        sizes = scratch[:, 2 * HALF : 3 * HALF]
        whole = scratch[:, 3 * HALF : 3 * HALF + REDUCED].bitcast(I32)

        warm = small.tile([P, 1], F32)
        nc.vector.memset(warm[:], 0.0)
        nc.scalar.activation(out=warm[:], in_=warm[:], func=ACT.Sin)

        one = small.tile([P, 1], F32)
        nc.vector.memset(one[:], 1.0)
        nc.vector.tensor_scalar_mul(turns[:, 0:1], one[:], SEQ / (2.0 * math.pi))
        n = 1
        while n < HALF:
            nc.vector.tensor_scalar_mul(turns[:, n : 2 * n], turns[:, 0:n], TURN_RATIO**n)
            n = 2 * n
        doubled = keep.tile([P, P], F32)
        nc.vector.tensor_copy(
            out=doubled[:].rearrange("p (m e) -> p m e", e=2),
            in_=turns[:, 0:64].unsqueeze(2).to_broadcast([P, 64, 2]),
        )
        first_column = fixed.tile([P, NT], F32, name="fixed2")
        nc.tensor.transpose(first_column[:, 0:128], doubled[:], ident[:])
        nc.vector.tensor_copy(out=whole, in_=turns[:, 0:REDUCED])
        nc.vector.tensor_tensor(out=turns[:, 0:REDUCED], in0=turns[:, 0:REDUCED], in1=whole, op=SUB)

        def sine(out, in_, sign):
            nc.scalar.activation(out=out, in_=in_, func=ACT.Sin, scale=sign * 2.0 * math.pi)

        def cosine(out, in_):
            nc.scalar.activation(out=out, in_=in_, func=ACT.Sin, scale=-2.0 * math.pi, bias=0.5 * math.pi)

        def table_bank(b):
            sine(sines[:, b, 0, :], turns[:, NT + P * b : NT + P * b + P], 1.0)
            sine(sines[:, b, 1, :], turns[:, P * b : P * b + P], -1.0)
            size = sizes[:, 256 * b : 256 * b + 256]
            nc.scalar.activation(out=size, in_=turns[:, 256 * b : 256 * b + 256], func=ACT.Abs)
            cosine(
                table[:, b, 0, :].rearrange("p (m e) -> p m e", e=2), size.unsqueeze(2).to_broadcast([P, 256, 2])
            )

        def widen_sines(b):
            nc.vector.tensor_copy(
                out=table[:, b, 1, :].rearrange("p (q h r) -> p q h r", h=2, r=2),
                in_=sines[:, b, :, :].rearrange("p r q -> p q r").unsqueeze(2).to_broadcast([P, P, 2, 2]),
            )

        angle = keep.tile([P, 16], F32)
        angle_whole = keep.tile([P, 16], I32)
        angle_size = keep.tile([P, 16], F32)
        trig = keep.tile([P, 2, 16], F32)

        def first_angle():
            nc.vector.tensor_copy(out=angle[:, 0:1], in_=first_column[:, 0:1])

        def more_angles(n):
            nc.vector.tensor_scalar_mul(angle[:, n : 2 * n], angle[:, 0:n], TURN_RATIO ** (64 * n))

        def reduce_angles():
            nc.vector.tensor_copy(out=angle_whole[:], in_=angle[:])
            nc.vector.tensor_tensor(out=angle[:], in0=angle[:], in1=angle_whole[:], op=SUB)
            sine(trig[:, 0, 0:8], angle[:, 0:8], -1.0)
            sine(trig[:, 0, 8:16], angle[:, 8:16], 1.0)
            nc.scalar.activation(out=angle_size[:], in_=angle[:], func=ACT.Abs)
            cosine(trig[:, 1, :], angle_size[:])

        b_nat32 = keep.tile([P, P], F32)
        b_rot32 = keep.tile([P, 2 * P], F32)
        table_bank(0)
        table_bank(1)
        nc.scalar.copy(out=b_nat32[:], in_=b_nat[:])
        nc.scalar.copy(out=b_rot32[:], in_=b_rot[:])
        table_bank(2)
        table_bank(3)
        widen_sines(0)
        first_angle()
        b_cols = keep.tile([P, 48], F32)
        mixed = keep.tile([P, 2, 16], F32)
        mixed_b = keep.tile([P, 2, 16], F32)
        bias_hi = keep.tile([P, 2, HALF], F32)
        bias_v = keep.tile([P, E], F32)
        bias_lo = {}
        flipped = {}

        def flip_bias():
            bank = fixed.tile([P, NT], F32, name="fixed3")
            nc.tensor.transpose(bank[:, 0:128], b_nat32[:], ident[:])
            nc.tensor.transpose(bank[:, 128:256], b_rot32[:, 1 : 2 * P : 2], ident[:])
            nc.tensor.transpose(bank[:, 256:384], b_rot32[:, 0 : 2 * P : 2], ident[:])
            flipped[0] = bank

        def mix_columns():
            bank = flipped[0]
            nc.vector.tensor_tensor(
                out=mixed[:], in0=bank[:, 0:32].rearrange("p (s t) -> p s t", s=2),
                in1=trig[:, 1, :].unsqueeze(1).to_broadcast([P, 2, 16]), op=MULT,
            )
            for h in range(2):
                nc.vector.tensor_tensor(
                    out=mixed_b[:, :, 8 * h : 8 * h + 8],
                    in0=bank[:, 128 + 128 * h : 144 + 128 * h].rearrange("p (s t) -> p s t", s=2),
                    in1=trig[:, 0, 8 * h : 8 * h + 8].unsqueeze(1).to_broadcast([P, 2, 8]), op=MULT,
                )
            nc.scalar.copy(out=b_cols[:], in_=bank[:, 0:48])
            nc.gpsimd.tensor_tensor(out=mixed[:], in0=mixed[:], in1=mixed_b[:], op=ADD)

        def spread(bank, cols, t0):
            for t in range(4):
                nc.tensor.transpose(
                    bank[:, 128 * t : 128 * t + 128], cols[:, t0 + t : t0 + t + 1].to_broadcast([P, P]), ident[:]
                )

        def spread_low(s, b):
            bank = fixed.tile([P, NT], F32, name="fixed%d" % LOW.index((s, b)))
            spread(bank, mixed[:, s, :], 4 * b)
            bias_lo[s, b] = bank

        def spread_high(s, b):
            bank = acc.tile([P, NT], F32, name="bank")
            spread(bank, mixed[:, s, :], 8 + 4 * b)
            nc.scalar.copy(out=bias_hi[:, s, NT * b : NT * b + NT], in_=bank[:])

        def spread_v(b):
            bank = acc.tile([P, NT], F32, name="bank")
            spread(bank, b_cols[:], 32 + 4 * b)
            nc.scalar.copy(out=bias_v[:, NT * b : NT * b + NT], in_=bank[:])

        def matmuls(tile, col):
            xi = 0 if P * tile < X_CHUNKS[1][0] else 1
            xo = P * tile - X_CHUNKS[xi][0]
            wi = [i for i, (c0, width) in enumerate(W_CHUNKS) if c0 <= col < c0 + width][0]
            wo = col - W_CHUNKS[wi][0]
            bank = acc.tile([P, NT], F32, name="bank")
            for g in range(G):
                nc.tensor.matmul_mx(
                    out=bank[:],
                    lhsT=x_codes[xi][:, g, 2 * xo : 2 * xo + 2 * P].bitcast(FP4X4),
                    lhsT_scale=x_planes[xi][:, g, xo : xo + P],
                    rhs=w_codes[wi][:, g, 2 * wo : 2 * wo + 2 * NT].bitcast(FP4X4),
                    rhs_scale=w_planes[wi][:, g, wo : wo + NT],
                    start=(g == 0),
                    stop=(g == G - 1),
                )
            return bank

        def product(pr, tile, s, b):
            bank = matmuls(tile, E * s + NT * b)
            nc.vector.tensor_tensor(
                out=pr[:, b, :, :], in0=bank[:].unsqueeze(1).to_broadcast([P, 2, NT]), in1=table[:, b, :, :], op=MULT
            )

        def place(b):
            return NT * b

        def add_low_bias(pr, s, b):
            a = pr[:, b, 0, :]
            nc.vector.tensor_tensor(out=a, in0=bias_lo[s, b][:], in1=a, op=ADD)

        def add_terms(engine, pr, z):
            for half in (1, 0):
                engine.tensor_tensor(
                    out=z[:, HALF * half : HALF * half + HALF].rearrange("p (b h k) -> p b h k", b=2, h=2),
                    in0=pr[:, 2 * half : 2 * half + 2, 0, :].rearrange("p b (h k) -> p b h k", h=2),
                    in1=pr[:, :, 1, 1 - half : NT : 2].rearrange("p (b h) k -> p b h k", h=2),
                    op=ADD,
                )

        def add_high_bias(engine, z, s):
            c0 = NT * len([1 for l in LOW if l[0] == s])
            engine.tensor_tensor(out=z[:, c0:E], in0=z[:, c0:E], in1=bias_hi[:, s, c0 - HALF : HALF], op=ADD)

        def store(z, tile, s):
            nc.sync.dma_start(out=outs[s][P * tile : P * tile + P, :], in_=z[:])

        def norm(z, tile, s):
            squares = junk.tile([P, E], BF16, name="squares")
            total = small.tile([P, 1], F32, name="total")
            factor = small.tile([P, 1], F32, name="factor")
            nc.scalar.activation(out=squares[:], in_=z[:], func=ACT.Square, accum_out=total[:])
            nc.scalar.activation(out=factor[:], in_=total[:], func=ACT.Relu, bias=-1e-24)
            nc.scalar.activation(out=factor[:], in_=factor[:], func=ACT.Abs_reciprocal_sqrt, bias=1e-24)
            nc.scalar.activation(out=z[:], in_=z[:], func=ACT.Copy, scale=factor[:])

        v_tiles = {}
        stores = []

        def value(tile, b):
            if b == 0:
                vt = vs.tile([P, E], F32, name="v_out")
                v_tiles[tile] = vt
            vt = v_tiles[tile]
            bank = matmuls(tile, 2 * E + NT * b)
            nc.vector.tensor_tensor(
                out=vt[:, NT * b : NT * b + NT], in0=bank[:], in1=bias_v[:, NT * b : NT * b + NT], op=ADD
            )
            if tile == TILES - 1:
                nc.sync.dma_start(
                    out=outs[2][P * tile : P * tile + P, NT * b : NT * b + NT], in_=vt[:, NT * b : NT * b + NT]
                )
            elif b == 3:
                nc.sync.dma_start(out=outs[2][P * tile : P * tile + P, :], in_=vt[:])
            if stores and tile == TILES - 1 and b in (0, 2):
                ze, te, se, early = stores.pop(0)
                store(ze, te, se)

        units = [(0, 0), (1, 0), (0, 1), (1, 1)] + [(t, s) for t in range(2, TILES) for s in range(2)]
        v_queue = [(t, b) for t in range(TILES) for b in range(4)]
        hooks = {
            (0, 0): [lambda: more_angles(1), lambda: widen_sines(1), lambda: more_angles(2)],
            (0, 1): [flip_bias, lambda: more_angles(4), lambda: widen_sines(2), lambda: more_angles(8), reduce_angles],
            (0, 2): [lambda: widen_sines(3), mix_columns],
        }

        def hook(n, b, f, *args):
            hooks.setdefault((n, b), []).append(lambda: f(*args))

        spreads = [(spread_high, 0, b) for b in range(2) if (0, b + 2) not in LOW]
        spreads += [(spread_high, 1, b) for b in range(2) if (1, b + 2) not in LOW]
        spreads += [(spread_low, s, b) for s, b in LOW if s == 1] + [(spread_low, s, b) for s, b in LOW if s == 0]
        places = [(1, 2), (1, 3), (2, 0), (2, 1), (2, 2), (2, 3), (3, 0), (3, 1)]
        for (f, s, b), at in zip(spreads, places):
            hook(*at, f, s, b)
        for b in range(4):
            hook(3, 2 + b // 2, spread_v, b)
        done_v = 0
        held = []
        N = len(units)
        for n, (t, s) in enumerate(units):
            pr = prod.tile([P, BANKS, 2, NT], F32, name="products")
            want = 0 if n < 4 else ((n + 1 - 4) * (len(v_queue) - 3)) // (N - 4)
            for b in range(4):
                product(pr, t, s, b)
                for f in hooks.get((n, b), []):
                    f()
                if n >= 3 and (s, b - 1) in LOW:
                    add_low_bias(pr, s, b - 1)
                if done_v < want and b in (1, 3):
                    value(*v_queue[done_v])
                    done_v += 1
            while done_v < want:
                value(*v_queue[done_v])
                done_v += 1
            z = zs.tile([P, E], F32, name="z")
            if n in VECTOR_UNITS:
                add_terms(nc.vector, pr, z)
                if done_v < len(v_queue) and n >= N - 2:
                    value(*v_queue[done_v])
                    done_v += 1
                add_high_bias(nc.vector, z, s)
            else:
                add_terms(nc.gpsimd, pr, z)
                if n == 0:
                    held.append((z, t, s))
                else:
                    for zh, th, sh in held:
                        add_high_bias(nc.gpsimd, zh, sh)
                    add_high_bias(nc.gpsimd, z, s)
                    held = []
            if n < 3:
                stores.append((z, t, s, True))
            else:
                if n == 3:
                    for ze, te, se, early in stores:
                        for b in [l[1] for l in LOW if l[0] == se]:
                            lo = ze[:, place(b) : place(b) + NT]
                            nc.vector.tensor_tensor(out=lo, in0=bias_lo[se, b][:], in1=lo, op=ADD)
                        norm(ze, te, se)
                if n < N - 1:
                    norm(z, t, s)
                    stores.append((z, t, s, False))
            while len(stores) > 2 and n > 3:
                ze, te, se, early = stores.pop(0)
                store(ze, te, se)

        while done_v < len(v_queue):
            value(*v_queue[done_v])
            done_v += 1
        for ze, te, se, early in stores:
            store(ze, te, se)
        squares = junk.tile([P, E], BF16, name="squares")
        sums = small.tile([P, 2], F32, name="sums")
        factor = small.tile([P, 1], F32, name="factor")
        for h in range(2):
            cols = slice(HALF * h, HALF * h + HALF)
            nc.scalar.activation(out=squares[:, cols], in_=z[:, cols], func=ACT.Square, accum_out=sums[:, h : h + 1])
        nc.scalar.activation(out=factor[:], in_=sums[:, 0:1], func=ACT.Identity, bias=sums[:, 1:2])
        nc.scalar.activation(out=factor[:], in_=factor[:], func=ACT.Relu, bias=-1e-24)
        nc.scalar.activation(out=factor[:], in_=factor[:], func=ACT.Abs_reciprocal_sqrt, bias=1e-24)
        nc.scalar.activation(out=z[:, 0:HALF], in_=z[:, 0:HALF], func=ACT.Copy, scale=factor[:])
        nc.vector.tensor_scalar_mul(z[:, HALF:E], z[:, HALF:E], factor[:])
        rows = slice(P * (TILES - 1), P * TILES)
        nc.sync.dma_start(out=outs[1][rows, HALF:E], in_=z[:, HALF:E])
        nc.sync.dma_start(out=outs[1][rows, 0:HALF], in_=z[:, 0:HALF])
